import numpy as np
import ml_dtypes


BF16 = ml_dtypes.bfloat16


def bf(x):
    return np.asarray(x, np.float32).astype(BF16)


def f64(x):
    return np.asarray(x).astype(np.float64)


E2M1 = np.array([0.0, 0.5, 1.0, 1.5, 2.0, 3.0, 4.0, 6.0, -0.0, -0.5, -1.0, -1.5, -2.0, -3.0, -4.0, -6.0])


def pack_weight(w, fmt):
    k, n = w.shape
    w = f64(bf(w)).reshape(k // 32, 32, n)
    amax = np.abs(w).max(1)
    if fmt == "e4m3":
        byte = np.frexp(amax)[1] - 1 + 127 - 7
    else:
        mant, ex = np.frexp(amax / 6.0)
        byte = np.where(mant > 0.5, ex, ex - 1) + 127
    byte = np.clip(np.where(amax > 0, byte, 1), 1, 254)
    scaled = (w * np.exp2(127.0 - byte)[:, None, :]).reshape(k, n).astype(np.float32)
    by_word = np.ascontiguousarray(scaled.reshape(k // 512, 128, 4, n).transpose(0, 1, 3, 2))
    if fmt == "e4m3":
        words = by_word.astype(ml_dtypes.float8_e4m3fn).view(np.uint8)
    else:
        c = by_word.astype(ml_dtypes.float4_e2m1fn).view(np.uint8) & 0xF
        words = c[..., 0::2] | (c[..., 1::2] << 4)
    return np.ascontiguousarray(words), np.ascontiguousarray(byte.astype(np.uint8).reshape(k // 512, 16, n))


def unpack_weight(words, scales, fmt):
    g, p, n, _ = words.shape
    if fmt == "e4m3":
        vals = np.ascontiguousarray(words).view(ml_dtypes.float8_e4m3fn).astype(np.float64)
    else:
        nib = np.empty((g, p, n, 4), np.uint8)
        nib[..., 0::2] = words & 0xF
        nib[..., 1::2] = words >> 4
        vals = E2M1[nib]
    vals = vals * np.repeat(np.exp2(scales.astype(np.float64) - 127.0), 8, axis=1)[..., None]
    return vals.transpose(0, 1, 3, 2).reshape(g * 512, n)

def pack4(w):
    words, scales = pack_weight(w, "e2m1")
    return words.reshape(words.shape[0], 128, -1), scales


def unpack4(words, scales):
    return unpack_weight(words.reshape(words.shape[0], 128, -1, 2), scales, "e2m1")


def kspread(k):
    return np.exp2(np.repeat(np.random.randint(-6, 7, k // 32), 32).astype(np.float64))


B, S, E, H, KVH, D = 1, 1024, 8192, 16, 4, 128


def rope(t, cos, sin):
    tr = t.reshape(t.shape[:-1] + (-1, 2))
    xr, xi = tr[..., 0], tr[..., 1]
    c = cos[None, :, None, :]
    n = sin[None, :, None, :]
    return np.stack([xr * c - xi * n, xr * n + xi * c], axis=-1).reshape(t.shape)


def setup_inputs():
    s = kspread(E)
    a = np.sqrt(2.0 / E)
    ang = np.outer(np.arange(S), 1.0 / (10000.0 ** (np.arange(0, D, 2) / D)))
    x = np.random.standard_normal((B, S, E)) * s
    x_words, x_scales = pack4(x.reshape(B * S, E).T)
    wq_words, wq_scales = pack4((np.random.standard_normal((H * D, E)) * a / s[None, :]).T)
    wk_words, wk_scales = pack4((np.random.standard_normal((KVH * D, E)) * a / s[None, :]).T)
    wv_words, wv_scales = pack4((np.random.standard_normal((KVH * D, E)) * a / s[None, :]).T)
    return {"x_words": x_words, "x_scales": x_scales,
            "wq_w_words": wq_words, "wq_w_scales": wq_scales,
            "wk_w_words": wk_words, "wk_w_scales": wk_scales,
            "wv_w_words": wv_words, "wv_w_scales": wv_scales,
            "freqs_cos": bf(np.cos(ang)), "freqs_sin": bf(np.sin(ang))}


def reference(x_words, x_scales, wq_w_words, wq_w_scales, wk_w_words, wk_w_scales, wv_w_words, wv_w_scales, freqs_cos, freqs_sin):
    xq = unpack4(x_words, x_scales).T.reshape(B, S, E)
    q = (xq @ unpack4(wq_w_words, wq_w_scales)).reshape(B, S, H, D)
    k = (xq @ unpack4(wk_w_words, wk_w_scales)).reshape(B, S, KVH, D)
    v = (xq @ unpack4(wv_w_words, wv_w_scales)).reshape(B, S, KVH, D)
    c, n = f64(freqs_cos), f64(freqs_sin)
    return rope(q, c, n), rope(k, c, n), v

@@ -1,0 +1,200 @@
+from contextlib import ExitStack
+
+import concourse.mybir as mybir
+
+F32 = mybir.dt.float32
+BF16 = mybir.dt.bfloat16
+U8 = mybir.dt.uint8
+I32 = mybir.dt.int32
+FP4X4 = mybir.dt.float4_e2m1fn_x4
+ALU = mybir.AluOpType
+
+P = 128
+PASSES = 16
+TOKENS = 1024
+M_TILES = 8
+N_TILE = 512
+N_BLOCKS = 6
+HEADS_PER_BLOCK = 4
+HALF = 64
+FLOPS = 2 * 1024 * 8192 * 3072
+
+FIRST_RUNS = ((0, 2), (2, 4), (4, 8), (8, 12), (12, 16))
+LATER_CHUNK = 4
+WARM = 8
+
+
+def tile_attention_pa_kernel(
+    tc,
+    x_words,
+    x_scales,
+    wq_w_words,
+    wq_w_scales,
+    wk_w_words,
+    wk_w_scales,
+    wv_w_words,
+    wv_w_scales,
+    freqs_cos,
+    freqs_sin,
+    out_0,
+    out_1,
+    out_2,
+):
+    nc = tc.nc
+
+    blocks = [(wq_w_words, wq_w_scales, N_TILE * n) for n in range(4)]
+    blocks.append((wk_w_words, wk_w_scales, 0))
+    blocks.append((wv_w_words, wv_w_scales, 0))
+    q_rows = out_0.rearrange("b s h d -> (b s) (h d)")
+    k_rows = out_1.rearrange("b s h d -> (b s) (h d)")
+    v_rows = out_2.rearrange("b s h d -> (b s) (h d)")
+
+    def out_view(m, n):
+        rows = slice(P * m, P * (m + 1))
+        if n < 4:
+            return q_rows[rows, N_TILE * n : N_TILE * (n + 1)]
+        if n == 4:
+            return k_rows[rows, :]
+        return v_rows[rows, :]
+
+    with ExitStack() as ctx:
+        keep = ctx.enter_context(tc.tile_pool(name="keep", bufs=1))
+        tmp = ctx.enter_context(tc.tile_pool(name="tmp", bufs=2))
+        res_pool = ctx.enter_context(tc.tile_pool(name="res", bufs=4))
+        psum = ctx.enter_context(tc.psum_pool(name="psum", bufs=8))
+        ctx.enter_context(tc.manual_schedule())
+
+        zero = keep.tile([P, N_TILE], BF16, name="zero")
+        nc.gpsimd.memset(zero[:], 0.0)
+        cos_raw = keep.tile([P, M_TILES, HALF], BF16, name="cos_raw")
+        sin_raw = keep.tile([P, M_TILES, HALF], BF16, name="sin_raw")
+        nc.gpsimd.dma_start(out=cos_raw[:], in_=freqs_cos.rearrange("(m p) j -> p m j", p=P))
+        nc.gpsimd.dma_start(out=sin_raw[:], in_=freqs_sin.rearrange("(m p) j -> p m j", p=P))
+
+        warm = psum.tile([P, N_TILE], F32, name="warm", tag="acc")
+        for i in range(WARM):
+            nc.tensor.matmul(out=warm[:], lhsT=zero[:, 0:P], rhs=zero[:], start=True, stop=True)
+
+        def load_scales(name, scales, g0, g1, c0, width):
+            plane = keep.tile([P, g1 - g0, width], U8, name=name, align_bytes=64)
+            nc.vector.memset(plane[:].rearrange("p g c -> p (g c)").bitcast(I32), 0)
+            for q in range(4):
+                nc.sync.dma_start(
+                    out=plane[32 * q : 32 * q + 4, :, :].bitcast(I32),
+                    in_=scales[g0:g1, 4 * q : 4 * q + 4, c0 : c0 + width].rearrange("g r c -> r g c").bitcast(I32),
+                )
+            return plane
+
+        def load_codes(name, words, g0, g1, c0, width):
+            codes = keep.tile([P, g1 - g0, 2 * width], U8, name=name, align_bytes=64)
+            nc.sync.dma_start(
+                out=codes[:].bitcast(I32),
+                in_=words[g0:g1, :, 2 * c0 : 2 * (c0 + width)].rearrange("g p b -> p g b").bitcast(I32),
+            )
+            return codes
+
+        x_codes = {}
+        x_planes = {}
+        w_codes = [{} for n in range(N_BLOCKS)]
+        w_planes = [{} for n in range(N_BLOCKS)]
+        for g0, g1 in FIRST_RUNS:
+            xp = load_scales("xs%d" % g0, x_scales, g0, g1, 0, TOKENS)
+            wp = load_scales("ws0_%d" % g0, blocks[0][1], g0, g1, 0, N_TILE)
+            for g in range(g0, g1):
+                x_planes[g] = (xp, g - g0)
+                w_planes[0][g] = (wp, g - g0)
+                w_codes[0][g] = (load_codes("wc0_%d" % g, blocks[0][0], g, g + 1, 0, N_TILE), 0)
+                x_codes[g] = (load_codes("xc%d" % g, x_words, g, g + 1, 0, TOKENS), 0)
+        for n in range(1, N_BLOCKS):
+            words, scales, c0 = blocks[n]
+            wp = load_scales("ws%d" % n, scales, 0, PASSES, c0, N_TILE)
+            for g0 in range(0, PASSES, LATER_CHUNK):
+                wc = load_codes("wc%d_%d" % (n, g0), words, g0, g0 + LATER_CHUNK, c0, N_TILE)
+                for g in range(g0, g0 + LATER_CHUNK):
+                    w_planes[n][g] = (wp, g)
+                    w_codes[n][g] = (wc, g - g0)
+
+        cos2 = keep.tile([P, M_TILES, HALF, 2], F32, name="cos2")
+        sin_pos = keep.tile([P, M_TILES, HALF], F32, name="sin_pos")
+        sin_neg = keep.tile([P, M_TILES, HALF], F32, name="sin_neg")
+        nc.vector.tensor_copy(out=cos2[:], in_=cos_raw[:].unsqueeze(3).to_broadcast([P, M_TILES, HALF, 2]))
+        nc.vector.tensor_copy(out=sin_pos[:], in_=sin_raw[:])
+        nc.vector.tensor_scalar(out=sin_neg[:], in0=sin_raw[:], scalar1=-1.0, scalar2=None, op0=ALU.mult)
+
+        def mx(acc, m, n, g, c0=0, width=N_TILE):
+            xc, xi = x_codes[g]
+            xp, xj = x_planes[g]
+            wc, wi = w_codes[n][g]
+            wp, wj = w_planes[n][g]
+            nc.tensor.matmul_mx(
+                out=acc[:],
+                lhsT=xc[:, xi, 2 * P * m : 2 * P * (m + 1)].bitcast(FP4X4),
+                lhsT_scale=xp[:, xj, P * m : P * (m + 1)],
+                rhs=wc[:, wi, 2 * c0 : 2 * (c0 + width)].bitcast(FP4X4),
+                rhs_scale=wp[:, wj, c0 : c0 + width],
+                start=(g == 0),
+                stop=(g == PASSES - 1),
+            )
+
+        def rope(acc, m, n):
+            pairs = acc[:].rearrange("p (a e) -> p a e", e=2)
+            by_head = "p (h j) -> p h j"
+            t2 = tmp.tile([P, 2, N_TILE // 2], F32, name="t2")
+            nc.vector.tensor_tensor(
+                out=t2[:, 0, :].rearrange(by_head, h=HEADS_PER_BLOCK),
+                in0=pairs[:, :, 1].rearrange(by_head, h=HEADS_PER_BLOCK),
+                in1=sin_neg[:, m, :].unsqueeze(1).to_broadcast([P, HEADS_PER_BLOCK, HALF]),
+                op=ALU.mult,
+            )
+            nc.vector.tensor_tensor(
+                out=t2[:, 1, :].rearrange(by_head, h=HEADS_PER_BLOCK),
+                in0=pairs[:, :, 0].rearrange(by_head, h=HEADS_PER_BLOCK),
+                in1=sin_pos[:, m, :].unsqueeze(1).to_broadcast([P, HEADS_PER_BLOCK, HALF]),
+                op=ALU.mult,
+            )
+            t1 = tmp.tile([P, N_TILE], F32, name="t1")
+            nc.vector.tensor_tensor(
+                out=t1[:].rearrange(by_head, h=HEADS_PER_BLOCK),
+                in0=acc[:].rearrange(by_head, h=HEADS_PER_BLOCK),
+                in1=cos2[:, m, :, :].rearrange("p j e -> p (j e)").unsqueeze(1).to_broadcast([P, HEADS_PER_BLOCK, 2 * HALF]),
+                op=ALU.mult,
+            )
+            res = res_pool.tile([P, N_TILE], F32, name="res")
+            nc.vector.tensor_tensor(
+                out=res[:].rearrange("p (a e) -> p a e", e=2),
+                in0=t1[:].rearrange("p (a e) -> p a e", e=2),
+                in1=t2[:].rearrange("p e a -> p a e"),
+                op=ALU.add,
+            )
+            nc.scalar.dma_start(out=out_view(m, n), in_=res[:])
+
+        accs = [psum.tile([P, N_TILE], F32, name="acc%d" % m, tag="acc") for m in range(M_TILES)]
+        for g in range(PASSES):
+            for m in range(M_TILES):
+                mx(accs[m], m, 0, g)
+        for m in range(M_TILES):
+            rope(accs[m], m, 0)
+
+        for n in range(1, N_BLOCKS):
+            for m in range(M_TILES):
+                if n == N_BLOCKS - 1 and m == M_TILES - 1:
+                    break
+                acc = psum.tile([P, N_TILE], F32, name="acc", tag="acc")
+                for g in range(PASSES):
+                    mx(acc, m, n, g)
+                if n < N_BLOCKS - 1:
+                    rope(acc, m, n)
+                else:
+                    res = res_pool.tile([P, N_TILE], F32, name="res")
+                    nc.scalar.copy(out=res[:], in_=acc[:])
+                    nc.scalar.dma_start(out=out_view(m, n), in_=res[:])
+
+        m, n = M_TILES - 1, N_BLOCKS - 1
+        half_w = N_TILE // 2
+        for h in range(2):
+            acc = psum.tile([P, half_w], F32, name="acc_half", tag="acc")
+            for g in range(PASSES):
+                mx(acc, m, n, g, c0=half_w * h, width=half_w)
+            res = res_pool.tile([P, half_w], F32, name="res_half", tag="res")
+            nc.vector.tensor_copy(out=res[:], in_=acc[:])
+            nc.sync.dma_start(out=out_view(m, n)[:, half_w * h : half_w * (h + 1)], in_=res[:])

@@ -11,16 +11,11 @@ ALU = mybir.AluOpType
 
 P = 128
 PASSES = 16
-TOKENS = 1024
 M_TILES = 8
 N_TILE = 512
-N_BLOCKS = 6
 HEADS_PER_BLOCK = 4
 HALF = 64
 FLOPS = 2 * 1024 * 8192 * 3072
-
-FIRST_RUNS = ((0, 2), (2, 4), (4, 8), (8, 12), (12, 16))
-LATER_CHUNK = 4
 WARM = 8
 
 
@@ -41,10 +36,6 @@ def tile_attention_pa_kernel(
     out_2,
 ):
     nc = tc.nc
-
-    blocks = [(wq_w_words, wq_w_scales, N_TILE * n) for n in range(4)]
-    blocks.append((wk_w_words, wk_w_scales, 0))
-    blocks.append((wv_w_words, wv_w_scales, 0))
     q_rows = out_0.rearrange("b s h d -> (b s) (h d)")
     k_rows = out_1.rearrange("b s h d -> (b s) (h d)")
     v_rows = out_2.rearrange("b s h d -> (b s) (h d)")
@@ -64,55 +55,72 @@ def tile_attention_pa_kernel(
         psum = ctx.enter_context(tc.psum_pool(name="psum", bufs=8))
         ctx.enter_context(tc.manual_schedule())
 
-        zero = keep.tile([P, N_TILE], BF16, name="zero")
-        nc.gpsimd.memset(zero[:], 0.0)
+        if WARM:
+            zero = keep.tile([P, N_TILE], BF16, name="zero")
+            nc.vector.memset(zero[:], 0.0)
+            warm = psum.tile([P, N_TILE], F32, name="warm", tag="acc")
+            for i in range(WARM):
+                nc.tensor.matmul(out=warm[:], lhsT=zero[:, 0:P], rhs=zero[:], start=True, stop=True)
+
+        def group(name, words, scales, c0, width):
+            return {"name": name, "words": words, "scales": scales, "c0": c0, "width": width, "codes": {}, "planes": {}}
+
+        x_groups = [group("x%d" % t, x_words, x_scales, 512 * t, 512) for t in range(2)]
+        q_groups = [group("q%d" % t, wq_w_words, wq_w_scales, 1024 * t, 1024) for t in range(2)]
+        k_group = group("k", wk_w_words, wk_w_scales, 0, 512)
+        v_group = group("v", wv_w_words, wv_w_scales, 0, 512)
+
+        def load_codes(grp, g0, g1, soft=False):
+            c0, width = grp["c0"], grp["width"]
+            codes = keep.tile([P, g1 - g0, 2 * width], U8, name="%s_c%d" % (grp["name"], g0), align_bytes=64)
+            src = grp["words"][g0:g1, :, 2 * c0 : 2 * (c0 + width)].rearrange("g p b -> p g b")
+            if soft:
+                nc.gpsimd.dma_start(out=codes[:].bitcast(F32), in_=src.bitcast(F32))
+            else:
+                nc.sync.dma_start(out=codes[:].bitcast(I32), in_=src.bitcast(I32))
+            for g in range(g0, g1):
+                grp["codes"][g] = (codes, g - g0)
+
+        def new_planes(grp, g0, g1):
+            plane = keep.tile([P, g1 - g0, grp["width"]], U8, name="%s_s%d" % (grp["name"], g0), align_bytes=64)
+            for g in range(g0, g1):
+                grp["planes"][g] = (plane, g - g0, 0)
+
+        def fill_planes(grp, g0, g1, rows):
+            plane = grp["planes"][g0][0]
+            half = grp["c0"] // grp["width"]
+            half_rows = grp["scales"].rearrange("g r (h c) -> (g r h) c", h=2)
+            for r in rows:
+                first = 2 * r + half
+                nc.sync.dma_start(
+                    out=plane[r:P:4, :, :].bitcast(I32),
+                    in_=half_rows[32 * g0 + first : 32 * g1 + first, :].rearrange("(g b) c -> b g c", b=32).bitcast(I32),
+                )
+
+        def load_planes_whole(grp, g0, g1):
+            new_planes(grp, g0, g1)
+            fill_planes(grp, g0, g1, range(4))
+
+        def zero_planes(name, passes, width):
+            plane = keep.tile([P, passes, width], U8, name=name, align_bytes=64)
+            nc.vector.memset(plane[:].rearrange("p g c -> p (g c)").bitcast(I32), 0)
+            return plane
+
+        def load_planes_rows(plane, scales, g0, g1, grps):
+            for q in range(4):
+                nc.sync.dma_start(
+                    out=plane[32 * q : 32 * q + 4, :, :].bitcast(I32),
+                    in_=scales[g0:g1, 4 * q : 4 * q + 4, :].rearrange("g r c -> r g c").bitcast(I32),
+                )
+            for grp in grps:
+                for g in range(g0, g1):
+                    grp["planes"][g] = (plane, g - g0, grp["c0"])
+
+        x0, q0 = x_groups[0], q_groups[0]
         cos_raw = keep.tile([P, M_TILES, HALF], BF16, name="cos_raw")
         sin_raw = keep.tile([P, M_TILES, HALF], BF16, name="sin_raw")
         nc.gpsimd.dma_start(out=cos_raw[:], in_=freqs_cos.rearrange("(m p) j -> p m j", p=P))
         nc.gpsimd.dma_start(out=sin_raw[:], in_=freqs_sin.rearrange("(m p) j -> p m j", p=P))
-
-        warm = psum.tile([P, N_TILE], F32, name="warm", tag="acc")
-        for i in range(WARM):
-            nc.tensor.matmul(out=warm[:], lhsT=zero[:, 0:P], rhs=zero[:], start=True, stop=True)
-
-        def load_scales(name, scales, g0, g1, c0, width):
-            plane = keep.tile([P, g1 - g0, width], U8, name=name, align_bytes=64)
-            nc.vector.memset(plane[:].rearrange("p g c -> p (g c)").bitcast(I32), 0)
-            for q in range(4):
-                nc.sync.dma_start(
-                    out=plane[32 * q : 32 * q + 4, :, :].bitcast(I32),
-                    in_=scales[g0:g1, 4 * q : 4 * q + 4, c0 : c0 + width].rearrange("g r c -> r g c").bitcast(I32),
-                )
-            return plane
-
-        def load_codes(name, words, g0, g1, c0, width):
-            codes = keep.tile([P, g1 - g0, 2 * width], U8, name=name, align_bytes=64)
-            nc.sync.dma_start(
-                out=codes[:].bitcast(I32),
-                in_=words[g0:g1, :, 2 * c0 : 2 * (c0 + width)].rearrange("g p b -> p g b").bitcast(I32),
-            )
-            return codes
-
-        x_codes = {}
-        x_planes = {}
-        w_codes = [{} for n in range(N_BLOCKS)]
-        w_planes = [{} for n in range(N_BLOCKS)]
-        for g0, g1 in FIRST_RUNS:
-            xp = load_scales("xs%d" % g0, x_scales, g0, g1, 0, TOKENS)
-            wp = load_scales("ws0_%d" % g0, blocks[0][1], g0, g1, 0, N_TILE)
-            for g in range(g0, g1):
-                x_planes[g] = (xp, g - g0)
-                w_planes[0][g] = (wp, g - g0)
-                w_codes[0][g] = (load_codes("wc0_%d" % g, blocks[0][0], g, g + 1, 0, N_TILE), 0)
-                x_codes[g] = (load_codes("xc%d" % g, x_words, g, g + 1, 0, TOKENS), 0)
-        for n in range(1, N_BLOCKS):
-            words, scales, c0 = blocks[n]
-            wp = load_scales("ws%d" % n, scales, 0, PASSES, c0, N_TILE)
-            for g0 in range(0, PASSES, LATER_CHUNK):
-                wc = load_codes("wc%d_%d" % (n, g0), words, g0, g0 + LATER_CHUNK, c0, N_TILE)
-                for g in range(g0, g0 + LATER_CHUNK):
-                    w_planes[n][g] = (wp, g)
-                    w_codes[n][g] = (wc, g - g0)
 
         cos2 = keep.tile([P, M_TILES, HALF, 2], F32, name="cos2")
         sin_pos = keep.tile([P, M_TILES, HALF], F32, name="sin_pos")
@@ -120,18 +128,56 @@ def tile_attention_pa_kernel(
         nc.vector.tensor_copy(out=cos2[:], in_=cos_raw[:].unsqueeze(3).to_broadcast([P, M_TILES, HALF, 2]))
         nc.vector.tensor_copy(out=sin_pos[:], in_=sin_raw[:])
         nc.vector.tensor_scalar(out=sin_neg[:], in0=sin_raw[:], scalar1=-1.0, scalar2=None, op0=ALU.mult)
+        x_last = zero_planes("x_last", 1, 1024)
+        q_last = zero_planes("q_last", 1, 2048)
+        k_planes = zero_planes("k_planes", PASSES, 512)
+        v_planes = zero_planes("v_planes", PASSES, 512)
+
+        new_planes(x0, 0, 2)
+        new_planes(q0, 0, 2)
+        fill_planes(x0, 0, 2, range(4))
+        fill_planes(q0, 0, 2, (0, 1))
+        load_codes(x0, 0, 1)
+        load_codes(q0, 0, 1)
+        fill_planes(q0, 0, 2, (2, 3))
+        load_codes(q0, 1, 2)
+        load_codes(x0, 1, 2)
+        for s0, s1 in ((2, 6), (6, 10), (10, 15)):
+            load_planes_whole(x0, s0, s1)
+            load_planes_whole(q0, s0, s1)
+            for g0 in range(s0, s1, 2):
+                load_codes(q0, g0, g0 + 2)
+                load_codes(x0, g0, g0 + 2)
+        load_planes_rows(x_last, x_scales, PASSES - 1, PASSES, x_groups)
+        load_planes_rows(q_last, wq_w_scales, PASSES - 1, PASSES, q_groups)
+        for grp in (x_groups[1], q_groups[1]):
+            load_planes_whole(grp, 0, PASSES - 1)
+            for g0 in range(0, PASSES, 4):
+                load_codes(grp, g0, g0 + 4)
+        for grp, plane in ((k_group, k_planes), (v_group, v_planes)):
+            load_planes_rows(plane, grp["scales"], 0, PASSES, [grp])
+            for g0 in range(0, PASSES, 4):
+                load_codes(grp, g0, g0 + 4)
 
         def mx(acc, m, n, g, c0=0, width=N_TILE):
-            xc, xi = x_codes[g]
-            xp, xj = x_planes[g]
-            wc, wi = w_codes[n][g]
-            wp, wj = w_planes[n][g]
+            xg = x_groups[m // 4]
+            xcol = P * (m % 4)
+            if n < 4:
+                wg = q_groups[n // 2]
+                wcol = N_TILE * (n % 2) + c0
+            else:
+                wg = k_group if n == 4 else v_group
+                wcol = c0
+            xc, xi = xg["codes"][g]
+            xp, xj, xoff = xg["planes"][g]
+            wc, wi = wg["codes"][g]
+            wp, wj, woff = wg["planes"][g]
             nc.tensor.matmul_mx(
                 out=acc[:],
-                lhsT=xc[:, xi, 2 * P * m : 2 * P * (m + 1)].bitcast(FP4X4),
-                lhsT_scale=xp[:, xj, P * m : P * (m + 1)],
-                rhs=wc[:, wi, 2 * c0 : 2 * (c0 + width)].bitcast(FP4X4),
-                rhs_scale=wp[:, wj, c0 : c0 + width],
+                lhsT=xc[:, xi, 2 * xcol : 2 * (xcol + P)].bitcast(FP4X4),
+                lhsT_scale=xp[:, xj, xoff + xcol : xoff + xcol + P],
+                rhs=wc[:, wi, 2 * wcol : 2 * (wcol + width)].bitcast(FP4X4),
+                rhs_scale=wp[:, wj, woff + wcol : woff + wcol + width],
                 start=(g == 0),
                 stop=(g == PASSES - 1),
             )
@@ -166,30 +212,30 @@ def tile_attention_pa_kernel(
                 in1=t2[:].rearrange("p e a -> p a e"),
                 op=ALU.add,
             )
-            nc.scalar.dma_start(out=out_view(m, n), in_=res[:])
+            nc.gpsimd.dma_start(out=out_view(m, n), in_=res[:])
 
-        accs = [psum.tile([P, N_TILE], F32, name="acc%d" % m, tag="acc") for m in range(M_TILES)]
+        first = [(m, n) for m in range(4) for n in range(2)]
+        accs = [psum.tile([P, N_TILE], F32, name="acc%d" % i, tag="acc") for i in range(8)]
         for g in range(PASSES):
-            for m in range(M_TILES):
-                mx(accs[m], m, 0, g)
-        for m in range(M_TILES):
-            rope(accs[m], m, 0)
+            for i in range(8):
+                mx(accs[i], first[i][0], first[i][1], g)
+        for i in range(8):
+            rope(accs[i], first[i][0], first[i][1])
 
-        for n in range(1, N_BLOCKS):
-            for m in range(M_TILES):
-                if n == N_BLOCKS - 1 and m == M_TILES - 1:
-                    break
-                acc = psum.tile([P, N_TILE], F32, name="acc", tag="acc")
-                for g in range(PASSES):
-                    mx(acc, m, n, g)
-                if n < N_BLOCKS - 1:
-                    rope(acc, m, n)
-                else:
-                    res = res_pool.tile([P, N_TILE], F32, name="res")
-                    nc.scalar.copy(out=res[:], in_=acc[:])
-                    nc.scalar.dma_start(out=out_view(m, n), in_=res[:])
+        rest = [(m, n) for m in range(4, 8) for n in range(2)]
+        rest.extend([(m, n) for n in range(2, 6) for m in range(M_TILES)])
+        for m, n in rest[:-1]:
+            acc = psum.tile([P, N_TILE], F32, name="acc", tag="acc")
+            for g in range(PASSES):
+                mx(acc, m, n, g)
+            if n < 5:
+                rope(acc, m, n)
+            else:
+                res = res_pool.tile([P, N_TILE], F32, name="res")
+                nc.scalar.copy(out=res[:], in_=acc[:])
+                nc.scalar.dma_start(out=out_view(m, n), in_=res[:])
 
-        m, n = M_TILES - 1, N_BLOCKS - 1
+        m, n = rest[-1]
         half_w = N_TILE // 2
         for h in range(2):
             acc = psum.tile([P, half_w], F32, name="acc_half", tag="acc")

@@ -133,21 +133,23 @@ def tile_attention_pa_kernel(
         k_planes = zero_planes("k_planes", PASSES, 512)
         v_planes = zero_planes("v_planes", PASSES, 512)
 
-        new_planes(x0, 0, 2)
-        new_planes(q0, 0, 2)
-        fill_planes(x0, 0, 2, range(4))
-        fill_planes(q0, 0, 2, (0, 1))
+        new_planes(x0, 0, 3)
+        new_planes(q0, 0, 3)
+        fill_planes(x0, 0, 3, (0, 1))
+        fill_planes(q0, 0, 3, range(4))
         load_codes(x0, 0, 1)
         load_codes(q0, 0, 1)
-        fill_planes(q0, 0, 2, (2, 3))
-        load_codes(q0, 1, 2)
-        load_codes(x0, 1, 2)
-        for s0, s1 in ((2, 6), (6, 10), (10, 15)):
+        fill_planes(x0, 0, 3, (2, 3))
+        for g in (1, 2):
+            load_codes(q0, g, g + 1)
+            load_codes(x0, g, g + 1)
+        for cuts in ((3, 4, 6, 8), (8, 10, 12), (12, 14, 16)):
+            s0, s1 = cuts[0], min(cuts[-1], PASSES - 1)
             load_planes_whole(x0, s0, s1)
             load_planes_whole(q0, s0, s1)
-            for g0 in range(s0, s1, 2):
-                load_codes(q0, g0, g0 + 2)
-                load_codes(x0, g0, g0 + 2)
+            for g0, g1 in zip(cuts, cuts[1:]):
+                load_codes(q0, g0, g1)
+                load_codes(x0, g0, g1)
         load_planes_rows(x_last, x_scales, PASSES - 1, PASSES, x_groups)
         load_planes_rows(q_last, wq_w_scales, PASSES - 1, PASSES, q_groups)
         for grp in (x_groups[1], q_groups[1]):

@@ -119,15 +119,6 @@ def tile_attention_pa_kernel(
         x0, q0 = x_groups[0], q_groups[0]
         cos_raw = keep.tile([P, M_TILES, HALF], BF16, name="cos_raw")
         sin_raw = keep.tile([P, M_TILES, HALF], BF16, name="sin_raw")
-        nc.gpsimd.dma_start(out=cos_raw[:], in_=freqs_cos.rearrange("(m p) j -> p m j", p=P))
-        nc.gpsimd.dma_start(out=sin_raw[:], in_=freqs_sin.rearrange("(m p) j -> p m j", p=P))
-
-        cos2 = keep.tile([P, M_TILES, HALF, 2], F32, name="cos2")
-        sin_pos = keep.tile([P, M_TILES, HALF], F32, name="sin_pos")
-        sin_neg = keep.tile([P, M_TILES, HALF], F32, name="sin_neg")
-        nc.vector.tensor_copy(out=cos2[:], in_=cos_raw[:].unsqueeze(3).to_broadcast([P, M_TILES, HALF, 2]))
-        nc.vector.tensor_copy(out=sin_pos[:], in_=sin_raw[:])
-        nc.vector.tensor_scalar(out=sin_neg[:], in0=sin_raw[:], scalar1=-1.0, scalar2=None, op0=ALU.mult)
         x_last = zero_planes("x_last", 1, 1024)
         q_last = zero_planes("q_last", 1, 2048)
         k_planes = zero_planes("k_planes", PASSES, 512)
@@ -150,6 +141,15 @@ def tile_attention_pa_kernel(
             for g0, g1 in zip(cuts, cuts[1:]):
                 load_codes(q0, g0, g1)
                 load_codes(x0, g0, g1)
+
+        nc.sync.dma_start(out=cos_raw[:], in_=freqs_cos.rearrange("(m p) j -> p m j", p=P))
+        nc.sync.dma_start(out=sin_raw[:], in_=freqs_sin.rearrange("(m p) j -> p m j", p=P))
+        cos2 = keep.tile([P, M_TILES, HALF, 2], F32, name="cos2")
+        sin_pos = keep.tile([P, M_TILES, HALF], F32, name="sin_pos")
+        sin_neg = keep.tile([P, M_TILES, HALF], F32, name="sin_neg")
+        nc.vector.tensor_copy(out=cos2[:], in_=cos_raw[:].unsqueeze(3).to_broadcast([P, M_TILES, HALF, 2]))
+        nc.vector.tensor_copy(out=sin_pos[:], in_=sin_raw[:])
+        nc.vector.tensor_scalar(out=sin_neg[:], in0=sin_raw[:], scalar1=-1.0, scalar2=None, op0=ALU.mult)
         load_planes_rows(x_last, x_scales, PASSES - 1, PASSES, x_groups)
         load_planes_rows(q_last, wq_w_scales, PASSES - 1, PASSES, q_groups)
         for grp in (x_groups[1], q_groups[1]):

@@ -16,7 +16,7 @@ N_TILE = 512
 HEADS_PER_BLOCK = 4
 HALF = 64
 FLOPS = 2 * 1024 * 8192 * 3072
-WARM = 8
+WARM = 6
 
 
 def tile_attention_pa_kernel(

@@ -138,6 +138,9 @@ def tile_attention_pa_kernel(
             s0, s1 = cuts[0], min(cuts[-1], PASSES - 1)
             load_planes_whole(x0, s0, s1)
             load_planes_whole(q0, s0, s1)
+            if cuts[-1] == PASSES:
+                load_planes_rows(x_last, x_scales, PASSES - 1, PASSES, x_groups)
+                load_planes_rows(q_last, wq_w_scales, PASSES - 1, PASSES, q_groups)
             for g0, g1 in zip(cuts, cuts[1:]):
                 load_codes(q0, g0, g1)
                 load_codes(x0, g0, g1)
@@ -150,16 +153,21 @@ def tile_attention_pa_kernel(
         nc.vector.tensor_copy(out=cos2[:], in_=cos_raw[:].unsqueeze(3).to_broadcast([P, M_TILES, HALF, 2]))
         nc.vector.tensor_copy(out=sin_pos[:], in_=sin_raw[:])
         nc.vector.tensor_scalar(out=sin_neg[:], in0=sin_raw[:], scalar1=-1.0, scalar2=None, op0=ALU.mult)
-        load_planes_rows(x_last, x_scales, PASSES - 1, PASSES, x_groups)
-        load_planes_rows(q_last, wq_w_scales, PASSES - 1, PASSES, q_groups)
-        for grp in (x_groups[1], q_groups[1]):
-            load_planes_whole(grp, 0, PASSES - 1)
-            for g0 in range(0, PASSES, 4):
-                load_codes(grp, g0, g0 + 4)
-        for grp, plane in ((k_group, k_planes), (v_group, v_planes)):
+
+        def load_rows_group(grp, plane):
             load_planes_rows(plane, grp["scales"], 0, PASSES, [grp])
             for g0 in range(0, PASSES, 4):
                 load_codes(grp, g0, g0 + 4)
+
+        def load_half_group(grp):
+            load_planes_whole(grp, 0, PASSES - 1)
+            for g0 in range(0, PASSES, 4):
+                load_codes(grp, g0, g0 + 4)
+
+        load_rows_group(k_group, k_planes)
+        load_half_group(x_groups[1])
+        load_half_group(q_groups[1])
+        load_rows_group(v_group, v_planes)
 
         def mx(acc, m, n, g, c0=0, width=N_TILE):
             xg = x_groups[m // 4]
@@ -224,8 +232,9 @@ def tile_attention_pa_kernel(
         for i in range(8):
             rope(accs[i], first[i][0], first[i][1])
 
-        rest = [(m, n) for m in range(4, 8) for n in range(2)]
-        rest.extend([(m, n) for n in range(2, 6) for m in range(M_TILES)])
+        rest = [(m, 4) for m in range(4)]
+        rest.extend([(m, n) for m in range(4, 8) for n in (0, 1, 4)])
+        rest.extend([(m, n) for n in (2, 3, 5) for m in range(M_TILES)])
         for m, n in rest[:-1]:
             acc = psum.tile([P, N_TILE], F32, name="acc", tag="acc")
             for g in range(PASSES):

@@ -226,9 +226,10 @@ def tile_attention_pa_kernel(
 
         first = [(m, n) for m in range(4) for n in range(2)]
         accs = [psum.tile([P, N_TILE], F32, name="acc%d" % i, tag="acc") for i in range(8)]
-        for g in range(PASSES):
+        for run in ((0,), (1,), (2,), (3,), (4, 5), (6, 7), (8, 9, 10, 11), (12, 13, 14, 15)):
             for i in range(8):
-                mx(accs[i], first[i][0], first[i][1], g)
+                for g in run:
+                    mx(accs[i], first[i][0], first[i][1], g)
         for i in range(8):
             rope(accs[i], first[i][0], first[i][1])
 

@@ -124,19 +124,22 @@ def tile_attention_pa_kernel(
         k_planes = zero_planes("k_planes", PASSES, 512)
         v_planes = zero_planes("v_planes", PASSES, 512)
 
-        new_planes(x0, 0, 3)
+        new_planes(x0, 0, 1)
         new_planes(q0, 0, 3)
-        fill_planes(x0, 0, 3, (0, 1))
+        fill_planes(x0, 0, 1, (0, 1))
         fill_planes(q0, 0, 3, range(4))
         load_codes(x0, 0, 1)
         load_codes(q0, 0, 1)
-        fill_planes(x0, 0, 3, (2, 3))
-        for g in (1, 2):
-            load_codes(q0, g, g + 1)
-            load_codes(x0, g, g + 1)
+        fill_planes(x0, 0, 1, (2, 3))
+        load_codes(q0, 1, 2)
+        load_codes(x0, 1, 2)
+        load_planes_whole(x0, 1, 8)
+        load_codes(q0, 2, 3)
+        load_codes(x0, 2, 3)
         for cuts in ((3, 4, 6, 8), (8, 10, 12), (12, 14, 16)):
             s0, s1 = cuts[0], min(cuts[-1], PASSES - 1)
-            load_planes_whole(x0, s0, s1)
+            if s0 > 3:
+                load_planes_whole(x0, s0, s1)
             load_planes_whole(q0, s0, s1)
             if cuts[-1] == PASSES:
                 load_planes_rows(x_last, x_scales, PASSES - 1, PASSES, x_groups)

@@ -53,7 +53,6 @@ def tile_attention_pa_kernel(
         tmp = ctx.enter_context(tc.tile_pool(name="tmp", bufs=2))
         res_pool = ctx.enter_context(tc.tile_pool(name="res", bufs=4))
         psum = ctx.enter_context(tc.psum_pool(name="psum", bufs=8))
-        ctx.enter_context(tc.manual_schedule())
 
         if WARM:
             zero = keep.tile([P, N_TILE], BF16, name="zero")

@@ -256,5 +256,5 @@ def tile_attention_pa_kernel(
             for g in range(PASSES):
                 mx(acc, m, n, g, c0=half_w * h, width=half_w)
             res = res_pool.tile([P, half_w], F32, name="res_half", tag="res")
-            nc.vector.tensor_copy(out=res[:], in_=acc[:])
-            nc.sync.dma_start(out=out_view(m, n)[:, half_w * h : half_w * (h + 1)], in_=res[:])
+            nc.scalar.copy(out=res[:], in_=acc[:])
+            nc.scalar.dma_start(out=out_view(m, n)[:, half_w * h : half_w * (h + 1)], in_=res[:])

@@ -250,11 +250,10 @@ def tile_attention_pa_kernel(
                 nc.scalar.dma_start(out=out_view(m, n), in_=res[:])
 
         m, n = rest[-1]
-        half_w = N_TILE // 2
-        for h in range(2):
-            acc = psum.tile([P, half_w], F32, name="acc_half", tag="acc")
+        for c0, part_w in ((0, 256), (256, 128), (384, 128)):
+            acc = psum.tile([P, part_w], F32, name="acc_half", tag="acc")
             for g in range(PASSES):
-                mx(acc, m, n, g, c0=half_w * h, width=half_w)
-            res = res_pool.tile([P, half_w], F32, name="res_half", tag="res")
+                mx(acc, m, n, g, c0=c0, width=part_w)
+            res = res_pool.tile([P, part_w], F32, name="res_half", tag="res")
             nc.scalar.copy(out=res[:], in_=acc[:])
-            nc.scalar.dma_start(out=out_view(m, n)[:, half_w * h : half_w * (h + 1)], in_=res[:])
+            nc.scalar.dma_start(out=out_view(m, n)[:, c0 : c0 + part_w], in_=res[:])

from contextlib import ExitStack

import concourse.mybir as mybir

F32 = mybir.dt.float32
BF16 = mybir.dt.bfloat16
U8 = mybir.dt.uint8
I32 = mybir.dt.int32
FP4X4 = mybir.dt.float4_e2m1fn_x4
ALU = mybir.AluOpType

P = 128
PASSES = 16
M_TILES = 8
N_TILE = 512
HEADS_PER_BLOCK = 4
HALF = 64
FLOPS = 2 * 1024 * 8192 * 3072
WARM = 6


def tile_attention_pa_kernel(
    tc,
    x_words,
    x_scales,
    wq_w_words,
    wq_w_scales,
    wk_w_words,
    wk_w_scales,
    wv_w_words,
    wv_w_scales,
    freqs_cos,
    freqs_sin,
    out_0,
    out_1,
    out_2,
):
    nc = tc.nc
    q_rows = out_0.rearrange("b s h d -> (b s) (h d)")
    k_rows = out_1.rearrange("b s h d -> (b s) (h d)")
    v_rows = out_2.rearrange("b s h d -> (b s) (h d)")

    def out_view(m, n):
        rows = slice(P * m, P * (m + 1))
        if n < 4:
            return q_rows[rows, N_TILE * n : N_TILE * (n + 1)]
        if n == 4:
            return k_rows[rows, :]
        return v_rows[rows, :]

    with ExitStack() as ctx:
        keep = ctx.enter_context(tc.tile_pool(name="keep", bufs=1))
        tmp = ctx.enter_context(tc.tile_pool(name="tmp", bufs=2))
        res_pool = ctx.enter_context(tc.tile_pool(name="res", bufs=4))
        psum = ctx.enter_context(tc.psum_pool(name="psum", bufs=8))

        if WARM:
            zero = keep.tile([P, N_TILE], BF16, name="zero")
            nc.vector.memset(zero[:], 0.0)
            warm = psum.tile([P, N_TILE], F32, name="warm", tag="acc")
            for i in range(WARM):
                nc.tensor.matmul(out=warm[:], lhsT=zero[:, 0:P], rhs=zero[:], start=True, stop=True)

        def group(name, words, scales, c0, width):
            return {"name": name, "words": words, "scales": scales, "c0": c0, "width": width, "codes": {}, "planes": {}}

        x_groups = [group("x%d" % t, x_words, x_scales, 512 * t, 512) for t in range(2)]
        q_groups = [group("q%d" % t, wq_w_words, wq_w_scales, 1024 * t, 1024) for t in range(2)]
        k_group = group("k", wk_w_words, wk_w_scales, 0, 512)
        v_group = group("v", wv_w_words, wv_w_scales, 0, 512)

        def load_codes(grp, g0, g1, soft=False):
            c0, width = grp["c0"], grp["width"]
            codes = keep.tile([P, g1 - g0, 2 * width], U8, name="%s_c%d" % (grp["name"], g0), align_bytes=64)
            src = grp["words"][g0:g1, :, 2 * c0 : 2 * (c0 + width)].rearrange("g p b -> p g b")
            if soft:
                nc.gpsimd.dma_start(out=codes[:].bitcast(F32), in_=src.bitcast(F32))
            else:
                nc.sync.dma_start(out=codes[:].bitcast(I32), in_=src.bitcast(I32))
            for g in range(g0, g1):
                grp["codes"][g] = (codes, g - g0)

        def new_planes(grp, g0, g1):
            plane = keep.tile([P, g1 - g0, grp["width"]], U8, name="%s_s%d" % (grp["name"], g0), align_bytes=64)
            for g in range(g0, g1):
                grp["planes"][g] = (plane, g - g0, 0)

        def fill_planes(grp, g0, g1, rows):
            plane = grp["planes"][g0][0]
            half = grp["c0"] // grp["width"]
            half_rows = grp["scales"].rearrange("g r (h c) -> (g r h) c", h=2)
            for r in rows:
                first = 2 * r + half
                nc.sync.dma_start(
                    out=plane[r:P:4, :, :].bitcast(I32),
                    in_=half_rows[32 * g0 + first : 32 * g1 + first, :].rearrange("(g b) c -> b g c", b=32).bitcast(I32),
                )

        def load_planes_whole(grp, g0, g1):
            new_planes(grp, g0, g1)
            fill_planes(grp, g0, g1, range(4))

        def zero_planes(name, passes, width):
            plane = keep.tile([P, passes, width], U8, name=name, align_bytes=64)
            nc.vector.memset(plane[:].rearrange("p g c -> p (g c)").bitcast(I32), 0)
            return plane

        def load_planes_rows(plane, scales, g0, g1, grps):
            for q in range(4):
                nc.sync.dma_start(
                    out=plane[32 * q : 32 * q + 4, :, :].bitcast(I32),
                    in_=scales[g0:g1, 4 * q : 4 * q + 4, :].rearrange("g r c -> r g c").bitcast(I32),
                )
            for grp in grps:
                for g in range(g0, g1):
                    grp["planes"][g] = (plane, g - g0, grp["c0"])

        x0, q0 = x_groups[0], q_groups[0]
        cos_raw = keep.tile([P, M_TILES, HALF], BF16, name="cos_raw")
        sin_raw = keep.tile([P, M_TILES, HALF], BF16, name="sin_raw")
        x_last = zero_planes("x_last", 1, 1024)
        q_last = zero_planes("q_last", 1, 2048)
        k_planes = zero_planes("k_planes", PASSES, 512)
        v_planes = zero_planes("v_planes", PASSES, 512)

        new_planes(x0, 0, 1)
        new_planes(q0, 0, 3)
        fill_planes(x0, 0, 1, (0, 1))
        fill_planes(q0, 0, 3, range(4))
        load_codes(x0, 0, 1)
        load_codes(q0, 0, 1)
        fill_planes(x0, 0, 1, (2, 3))
        load_codes(q0, 1, 2)
        load_codes(x0, 1, 2)
        load_planes_whole(x0, 1, 8)
        load_codes(q0, 2, 3)
        load_codes(x0, 2, 3)
        for cuts in ((3, 4, 6, 8), (8, 10, 12), (12, 14, 16)):
            s0, s1 = cuts[0], min(cuts[-1], PASSES - 1)
            if s0 > 3:
                load_planes_whole(x0, s0, s1)
            load_planes_whole(q0, s0, s1)
            if cuts[-1] == PASSES:
                load_planes_rows(x_last, x_scales, PASSES - 1, PASSES, x_groups)
                load_planes_rows(q_last, wq_w_scales, PASSES - 1, PASSES, q_groups)
            for g0, g1 in zip(cuts, cuts[1:]):
                load_codes(q0, g0, g1)
                load_codes(x0, g0, g1)

        nc.sync.dma_start(out=cos_raw[:], in_=freqs_cos.rearrange("(m p) j -> p m j", p=P))
        nc.sync.dma_start(out=sin_raw[:], in_=freqs_sin.rearrange("(m p) j -> p m j", p=P))
        cos2 = keep.tile([P, M_TILES, HALF, 2], F32, name="cos2")
        sin_pos = keep.tile([P, M_TILES, HALF], F32, name="sin_pos")
        sin_neg = keep.tile([P, M_TILES, HALF], F32, name="sin_neg")
        nc.vector.tensor_copy(out=cos2[:], in_=cos_raw[:].unsqueeze(3).to_broadcast([P, M_TILES, HALF, 2]))
        nc.vector.tensor_copy(out=sin_pos[:], in_=sin_raw[:])
        nc.vector.tensor_scalar(out=sin_neg[:], in0=sin_raw[:], scalar1=-1.0, scalar2=None, op0=ALU.mult)

        def load_rows_group(grp, plane):
            load_planes_rows(plane, grp["scales"], 0, PASSES, [grp])
            for g0 in range(0, PASSES, 4):
                load_codes(grp, g0, g0 + 4)

        def load_half_group(grp):
            load_planes_whole(grp, 0, PASSES - 1)
            for g0 in range(0, PASSES, 4):
                load_codes(grp, g0, g0 + 4)

        load_rows_group(k_group, k_planes)
        load_half_group(x_groups[1])
        load_half_group(q_groups[1])
        load_rows_group(v_group, v_planes)

        def mx(acc, m, n, g, c0=0, width=N_TILE):
            xg = x_groups[m // 4]
            xcol = P * (m % 4)
            if n < 4:
                wg = q_groups[n // 2]
                wcol = N_TILE * (n % 2) + c0
            else:
                wg = k_group if n == 4 else v_group
                wcol = c0
            xc, xi = xg["codes"][g]
            xp, xj, xoff = xg["planes"][g]
            wc, wi = wg["codes"][g]
            wp, wj, woff = wg["planes"][g]
            nc.tensor.matmul_mx(
                out=acc[:],
                lhsT=xc[:, xi, 2 * xcol : 2 * (xcol + P)].bitcast(FP4X4),
                lhsT_scale=xp[:, xj, xoff + xcol : xoff + xcol + P],
                rhs=wc[:, wi, 2 * wcol : 2 * (wcol + width)].bitcast(FP4X4),
                rhs_scale=wp[:, wj, woff + wcol : woff + wcol + width],
                start=(g == 0),
                stop=(g == PASSES - 1),
            )

        def rope(acc, m, n):
            pairs = acc[:].rearrange("p (a e) -> p a e", e=2)
            by_head = "p (h j) -> p h j"
            t2 = tmp.tile([P, 2, N_TILE // 2], F32, name="t2")
            nc.vector.tensor_tensor(
                out=t2[:, 0, :].rearrange(by_head, h=HEADS_PER_BLOCK),
                in0=pairs[:, :, 1].rearrange(by_head, h=HEADS_PER_BLOCK),
                in1=sin_neg[:, m, :].unsqueeze(1).to_broadcast([P, HEADS_PER_BLOCK, HALF]),
                op=ALU.mult,
            )
            nc.vector.tensor_tensor(
                out=t2[:, 1, :].rearrange(by_head, h=HEADS_PER_BLOCK),
                in0=pairs[:, :, 0].rearrange(by_head, h=HEADS_PER_BLOCK),
                in1=sin_pos[:, m, :].unsqueeze(1).to_broadcast([P, HEADS_PER_BLOCK, HALF]),
                op=ALU.mult,
            )
            t1 = tmp.tile([P, N_TILE], F32, name="t1")
            nc.vector.tensor_tensor(
                out=t1[:].rearrange(by_head, h=HEADS_PER_BLOCK),
                in0=acc[:].rearrange(by_head, h=HEADS_PER_BLOCK),
                in1=cos2[:, m, :, :].rearrange("p j e -> p (j e)").unsqueeze(1).to_broadcast([P, HEADS_PER_BLOCK, 2 * HALF]),
                op=ALU.mult,
            )
            res = res_pool.tile([P, N_TILE], F32, name="res")
            nc.vector.tensor_tensor(
                out=res[:].rearrange("p (a e) -> p a e", e=2),
                in0=t1[:].rearrange("p (a e) -> p a e", e=2),
                in1=t2[:].rearrange("p e a -> p a e"),
                op=ALU.add,
            )
            nc.gpsimd.dma_start(out=out_view(m, n), in_=res[:])

        first = [(m, n) for m in range(4) for n in range(2)]
        accs = [psum.tile([P, N_TILE], F32, name="acc%d" % i, tag="acc") for i in range(8)]
        for run in ((0,), (1,), (2,), (3,), (4, 5), (6, 7), (8, 9, 10, 11), (12, 13, 14, 15)):
            for i in range(8):
                for g in run:
                    mx(accs[i], first[i][0], first[i][1], g)
        for i in range(8):
            rope(accs[i], first[i][0], first[i][1])

        rest = [(m, 4) for m in range(4)]
        rest.extend([(m, n) for m in range(4, 8) for n in (0, 1, 4)])
        rest.extend([(m, n) for n in (2, 3, 5) for m in range(M_TILES)])
        for m, n in rest[:-1]:
            acc = psum.tile([P, N_TILE], F32, name="acc", tag="acc")
            for g in range(PASSES):
                mx(acc, m, n, g)
            if n < 5:
                rope(acc, m, n)
            else:
                res = res_pool.tile([P, N_TILE], F32, name="res")
                nc.scalar.copy(out=res[:], in_=acc[:])
                nc.scalar.dma_start(out=out_view(m, n), in_=res[:])

        m, n = rest[-1]
        for c0, part_w in ((0, 256), (256, 128), (384, 128)):
            acc = psum.tile([P, part_w], F32, name="acc_half", tag="acc")
            for g in range(PASSES):
                mx(acc, m, n, g, c0=c0, width=part_w)
            res = res_pool.tile([P, part_w], F32, name="res_half", tag="res")
            nc.scalar.copy(out=res[:], in_=acc[:])
            nc.scalar.dma_start(out=out_view(m, n)[:, c0 : c0 + part_w], in_=res[:])
